import numpy as np
import ml_dtypes


def mxq(x, axis, fmt="e4m3"):
    dtype, down = {"e4m3": (ml_dtypes.float8_e4m3fn, 7), "e5m2": (ml_dtypes.float8_e5m2, 14)}[fmt]
    v = np.moveaxis(np.asarray(x, np.float32).astype(ml_dtypes.bfloat16).astype(np.float64), axis, -1)
    blocks = v.reshape(v.shape[:-1] + (-1, 32))
    amax = np.abs(blocks).max(-1, keepdims=True)
    byte = np.maximum(np.where(amax > 0, np.frexp(amax)[1] - 1 + 127, 0) - down, 1)
    scale = np.exp2(byte - 127.0)
    codes = (blocks / scale).astype(np.float32).astype(dtype).astype(np.float64)
    return np.moveaxis((codes * scale).reshape(v.shape), -1, axis)


WIDE = False


def mx_kscale(k):
    if not WIDE:
        return np.ones(k)
    levels = np.array([10, -10, 5, -5, 0])
    a = np.random.permutation(np.resize(levels, k // 512 * 4)).reshape(k // 512, 4)
    idx = np.arange(k)
    return np.exp2(a[idx // 512, idx % 128 // 32])


BF16 = ml_dtypes.bfloat16


def bf(x):
    return np.asarray(x, np.float32).astype(BF16)


def f64(x):
    return np.asarray(x).astype(np.float64)


E2M1 = np.array([0.0, 0.5, 1.0, 1.5, 2.0, 3.0, 4.0, 6.0, -0.0, -0.5, -1.0, -1.5, -2.0, -3.0, -4.0, -6.0])


def pack_weight(w, fmt):
    k, n = w.shape
    w = f64(bf(w)).reshape(k // 32, 32, n)
    amax = np.abs(w).max(1)
    if fmt == "e4m3":
        byte = np.frexp(amax)[1] - 1 + 127 - 7
    else:
        mant, ex = np.frexp(amax / 6.0)
        byte = np.where(mant > 0.5, ex, ex - 1) + 127
    byte = np.clip(np.where(amax > 0, byte, 1), 1, 254)
    scaled = (w * np.exp2(127.0 - byte)[:, None, :]).reshape(k, n).astype(np.float32)
    by_word = np.ascontiguousarray(scaled.reshape(k // 512, 128, 4, n).transpose(0, 1, 3, 2))
    if fmt == "e4m3":
        words = by_word.astype(ml_dtypes.float8_e4m3fn).view(np.uint8)
    else:
        c = by_word.astype(ml_dtypes.float4_e2m1fn).view(np.uint8) & 0xF
        words = c[..., 0::2] | (c[..., 1::2] << 4)
    return np.ascontiguousarray(words), np.ascontiguousarray(byte.astype(np.uint8).reshape(k // 512, 16, n))


def unpack_weight(words, scales, fmt):
    g, p, n, _ = words.shape
    if fmt == "e4m3":
        vals = np.ascontiguousarray(words).view(ml_dtypes.float8_e4m3fn).astype(np.float64)
    else:
        nib = np.empty((g, p, n, 4), np.uint8)
        nib[..., 0::2] = words & 0xF
        nib[..., 1::2] = words >> 4
        vals = E2M1[nib]
    vals = vals * np.repeat(np.exp2(scales.astype(np.float64) - 127.0), 8, axis=1)[..., None]
    return vals.transpose(0, 1, 3, 2).reshape(g * 512, n)

def pack4(w):
    words, scales = pack_weight(w, "e2m1")
    return words.reshape(words.shape[0], 128, -1), scales


def unpack4(words, scales):
    return unpack_weight(words.reshape(words.shape[0], 128, -1, 2), scales, "e2m1")


B, C, IN, H, ND, NG, NL = 4, 128, 1024, 512, 2, 4, 2
N = B * C
USED = [0, 2, 3]


def sigmoid(v):
    return 1.0 / (1.0 + np.exp(-v))


def cell(inq, wt, b1, b2):
    wu = wt.reshape(-1, NG, H)[:, USED].reshape(-1, len(USED) * H)
    gates = (inq @ wu) + b1.reshape(NG, H)[USED].reshape(-1) + b2.reshape(NG, H)[USED].reshape(-1)
    i, g, o = np.split(gates, len(USED), axis=-1)
    c = sigmoid(i) * np.tanh(g)
    return sigmoid(o) * np.tanh(c)


def setup_inputs():
    s = mx_kscale(IN)
    x = bf(np.random.standard_normal((B, C, IN)) * s)
    w = np.random.standard_normal((ND, NG * H, IN)) * 1.5 / np.sqrt(IN) / s
    cat = np.ascontiguousarray(w.swapaxes(1, 2)).reshape(-1, NG * H)
    words, scales = pack4(cat)
    return {"x": x,
            "w_ih_words": words,
            "w_ih_scales": scales,
            "b_ih": bf(np.random.standard_normal((ND, NG * H)) * 0.3),
            "b_hh": bf(np.random.standard_normal((ND, NG * H)) * 0.3)}


def reference(x, w_ih_words, w_ih_scales, b_ih, b_hh):
    xq = mxq(f64(x).reshape(N, IN), 1, "e4m3")
    w = unpack4(w_ih_words, w_ih_scales).reshape(ND, IN, NG * H)
    b1, b2 = f64(b_ih), f64(b_hh)
    return np.concatenate([cell(xq, w[d], b1[d], b2[d]) for d in range(ND)], axis=-1)

@@ -1,0 +1,186 @@
+from contextlib import ExitStack
+
+import concourse.mybir as mybir
+from concourse.masks import make_identity
+
+F32 = mybir.dt.float32
+BF16 = mybir.dt.bfloat16
+I32 = mybir.dt.int32
+U32 = mybir.dt.uint32
+U8 = mybir.dt.uint8
+FP8X4 = mybir.dt.float8_e4m3fn_x4
+FP4X4 = mybir.dt.float4_e2m1fn_x4
+ACT = mybir.ActivationFunctionType
+ALU = mybir.AluOpType
+
+P = 128
+ROW_BLOCKS = 4
+ROWS = ROW_BLOCKS * P
+FEATURES = 1024
+K_PASS = 4 * P
+PASSES = FEATURES // K_PASS
+DIRECTIONS = 2
+HIDDEN = 512
+GATE_COLS = 4 * HIDDEN
+GATE_I, GATE_G, GATE_O = 0, 2, 3
+H_BLOCKS = HIDDEN // P
+UNITS = DIRECTIONS * H_BLOCKS
+
+FLOPS = 2 * ROWS * FEATURES * 3 * HIDDEN * DIRECTIONS
+BYTES = (
+    ROWS * FEATURES * 2
+    + DIRECTIONS * FEATURES * 3 * HIDDEN // 2
+    + DIRECTIONS * FEATURES * 3 * HIDDEN // 32
+    + 2 * DIRECTIONS * 3 * HIDDEN * 2
+    + ROWS * DIRECTIONS * HIDDEN * 4
+)
+
+
+def tile_lstmnetwork_pa_e_kernel(tc, x, w_ih_words, w_ih_scales, b_ih, b_hh, out):
+    nc = tc.nc
+    with ExitStack() as stack:
+        stack.enter_context(tc.manual_schedule())
+        keep = stack.enter_context(tc.tile_pool(name="keep", bufs=1))
+        work = stack.enter_context(tc.tile_pool(name="work", bufs=3))
+        gate_banks = stack.enter_context(tc.psum_pool(name="gate_banks", bufs=2))
+        flip_banks = stack.enter_context(tc.psum_pool(name="flip_banks", bufs=2))
+
+        bias_rows = keep.tile([P, 2, P], BF16)
+        nc.vector.memset(bias_rows[:], 0.0)
+        table_warmer = keep.tile([P, 1], F32)
+        nc.vector.memset(table_warmer[:], 0.0)
+        w_scales = keep.tile([P, DIRECTIONS * PASSES, GATE_COLS], U8, align_bytes=64)
+        nc.vector.memset(w_scales[:].bitcast(I32), 0)
+
+        nc.scalar.dma_start(out=bias_rows[0:32, 0, :], in_=b_ih.rearrange("d (s p) -> (d s) p", p=P))
+        nc.scalar.dma_start(out=bias_rows[0:32, 1, :], in_=b_hh.rearrange("d (s p) -> (d s) p", p=P))
+        nc.scalar.activation(out=table_warmer[:], in_=table_warmer[:], func=ACT.Sigmoid)
+
+        identity = keep.tile([P, P], F32)
+        make_identity(nc, identity[:])
+
+        x_rows = keep.tile([P, ROW_BLOCKS, FEATURES], BF16)
+        for r in range(ROW_BLOCKS):
+            nc.sync.dma_start(out=x_rows[:, r, :], in_=x[r])
+
+        w_words = keep.tile([P, DIRECTIONS * PASSES, 2 * GATE_COLS], U8, align_bytes=64)
+        for d in range(DIRECTIONS):
+            groups = slice(PASSES * d, PASSES * (d + 1))
+            for q in range(8):
+                first = 32 * (q // 4) + q % 4
+                nc.sync.dma_start(
+                    out=w_scales[first:P:64, groups, :].bitcast(I32),
+                    in_=w_ih_scales[groups, q:16:8, :].rearrange("g q n -> q g n").bitcast(I32),
+                )
+            for first_gate, last_gate in ((GATE_I, GATE_I), (GATE_G, GATE_O)):
+                some_bytes = slice(2 * HIDDEN * first_gate, 2 * HIDDEN * (last_gate + 1))
+                nc.sync.dma_start(
+                    out=w_words[:, groups, some_bytes].bitcast(I32),
+                    in_=w_ih_words[groups, :, some_bytes].rearrange("g p b -> p g b").bitcast(I32),
+                )
+
+        bias_sum_rows = keep.tile([P, P], F32)
+        nc.vector.tensor_tensor(
+            out=bias_sum_rows[:], in0=bias_rows[:, 0, :], in1=bias_rows[:, 1, :], op=ALU.add
+        )
+
+        x_grouped = keep.tile([P, PASSES, ROWS, 4], BF16, align_bytes=64)
+        x_codes = keep.tile([P, PASSES, ROWS], U32, align_bytes=64)
+        x_scales = keep.tile([P, PASSES, ROWS], U8, align_bytes=64)
+        for r in range(ROW_BLOCKS):
+            rows = slice(P * r, P * (r + 1))
+            word_cols = x_rows[:, r, :].bitcast(F32)
+            for c in range(PASSES):
+                flipped_x = flip_banks.tile([P, 2, P], F32, tag="flip")
+                for u in range(2):
+                    nc.tensor.transpose(
+                        flipped_x[:, u, :], word_cols[:, 256 * c + u : 256 * (c + 1) : 2], identity[:]
+                    )
+                nc.scalar.copy(
+                    out=x_grouped[:, c, rows, :].bitcast(F32),
+                    in_=flipped_x[:].rearrange("p u r -> p r u"),
+                )
+                nc.vector.quantize_mx(
+                    out=x_codes[:, c, rows].bitcast(FP8X4),
+                    scales=x_scales[:, c, rows],
+                    in_=x_grouped[:, c, rows, :].rearrange("p r t -> p (r t)"),
+                )
+
+        flipped_bias = flip_banks.tile([P, P], F32, tag="flip")
+        nc.tensor.transpose(flipped_bias[:], bias_sum_rows[:], identity[:])
+        bias_cols = keep.tile([P, 32], F32)
+        nc.vector.tensor_copy(out=bias_cols[:], in_=flipped_bias[:, 0:32])
+
+        out_blocks = out.rearrange("(r p) n -> p r n", p=P)
+        sums = {}
+        parts = {}
+
+        def bias_of(unit, gate):
+            d, j = divmod(unit, H_BLOCKS)
+            col = 16 * d + 4 * gate + j
+            return bias_cols[:, col : col + 1]
+
+        def multiply(unit):
+            d, j = divmod(unit, H_BLOCKS)
+            for gate in (GATE_I, GATE_G, GATE_O):
+                n0 = HIDDEN * gate + P * j
+                bank = gate_banks.tile([P, ROWS], F32, name="bank", tag="gate%d" % gate)
+                for c in range(PASSES):
+                    g = PASSES * d + c
+                    nc.tensor.matmul_mx(
+                        out=bank[:],
+                        lhsT=w_words[:, g, 2 * n0 : 2 * (n0 + P)].bitcast(FP4X4),
+                        lhsT_scale=w_scales[:, g, n0 : n0 + P],
+                        rhs=x_codes[:, c, :].bitcast(FP8X4),
+                        rhs_scale=x_scales[:, c, :],
+                        start=(c == 0),
+                        stop=(c == PASSES - 1),
+                    )
+                sums[unit, gate] = bank
+
+        def squash(unit, gate, func, name):
+            result = work.tile([P, ROWS], F32, name=name, tag=name)
+            nc.scalar.activation(out=result[:], in_=sums[unit, gate][:], func=func, bias=bias_of(unit, gate))
+            parts[unit, name] = result
+
+        def product(unit, name, left, right):
+            result = work.tile([P, ROWS], F32, name=name, tag=name)
+            nc.vector.tensor_tensor(
+                out=result[:], in0=parts[unit, left][:], in1=parts[unit, right][:], op=ALU.mult
+            )
+            parts[unit, name] = result
+
+        def cell_state(unit):
+            squash(unit, GATE_I, ACT.Sigmoid, "sig_i")
+            squash(unit, GATE_G, ACT.Tanh, "tanh_g")
+            product(unit, "cell", "sig_i", "tanh_g")
+
+        def hidden_state(unit):
+            tanh_c = work.tile([P, ROWS], F32)
+            nc.scalar.activation(out=tanh_c[:], in_=parts[unit, "cell"][:], func=ACT.Tanh)
+            parts[unit, "tanh_c"] = tanh_c
+            product(unit, "hidden", "sig_o", "tanh_c")
+
+        def turn_and_store(unit):
+            flipped_h = flip_banks.tile([P, ROW_BLOCKS, P], F32, tag="flip")
+            for r in range(ROW_BLOCKS):
+                nc.tensor.transpose(
+                    flipped_h[:, r, :], parts[unit, "hidden"][:, P * r : P * (r + 1)], identity[:]
+                )
+            h_rows = work.tile([P, ROW_BLOCKS, P], F32)
+            nc.vector.tensor_copy(out=h_rows[:], in_=flipped_h[:])
+            nc.sync.dma_start(out=out_blocks[:, :, P * unit : P * (unit + 1)], in_=h_rows[:])
+
+        multiply(0)
+        multiply(1)
+        for unit in range(UNITS + 1):
+            if unit < UNITS:
+                cell_state(unit)
+            if unit > 0:
+                hidden_state(unit - 1)
+            if unit < UNITS:
+                squash(unit, GATE_O, ACT.Sigmoid, "sig_o")
+            if unit + 2 < UNITS:
+                multiply(unit + 2)
+            if unit > 0:
+                turn_and_store(unit - 1)

@@ -161,26 +161,31 @@ def tile_lstmnetwork_pa_e_kernel(tc, x, w_ih_words, w_ih_scales, b_ih, b_hh, out
             parts[unit, "tanh_c"] = tanh_c
             product(unit, "hidden", "sig_o", "tanh_c")
 
-        def turn_and_store(unit):
+        def turn(unit):
             flipped_h = flip_banks.tile([P, ROW_BLOCKS, P], F32, tag="flip")
             for r in range(ROW_BLOCKS):
                 nc.tensor.transpose(
                     flipped_h[:, r, :], parts[unit, "hidden"][:, P * r : P * (r + 1)], identity[:]
                 )
+            parts[unit, "flipped_h"] = flipped_h
+
+        def store(unit):
             h_rows = work.tile([P, ROW_BLOCKS, P], F32)
-            nc.vector.tensor_copy(out=h_rows[:], in_=flipped_h[:])
+            nc.vector.tensor_copy(out=h_rows[:], in_=parts[unit, "flipped_h"][:])
             nc.sync.dma_start(out=out_blocks[:, :, P * unit : P * (unit + 1)], in_=h_rows[:])
 
         multiply(0)
         multiply(1)
-        for unit in range(UNITS + 1):
-            if unit < UNITS:
-                cell_state(unit)
-            if unit > 0:
-                hidden_state(unit - 1)
-            if unit < UNITS:
-                squash(unit, GATE_O, ACT.Sigmoid, "sig_o")
-            if unit + 2 < UNITS:
-                multiply(unit + 2)
-            if unit > 0:
-                turn_and_store(unit - 1)
+        for step in range(UNITS + 2):
+            if step < UNITS:
+                cell_state(step)
+            if 1 <= step <= UNITS:
+                hidden_state(step - 1)
+            if step < UNITS:
+                squash(step, GATE_O, ACT.Sigmoid, "sig_o")
+            if step + 2 < UNITS:
+                multiply(step + 2)
+            if 1 <= step <= UNITS:
+                turn(step - 1)
+            if step >= 2:
+                store(step - 2)

@@ -25,6 +25,7 @@ GATE_COLS = 4 * HIDDEN
 GATE_I, GATE_G, GATE_O = 0, 2, 3
 H_BLOCKS = HIDDEN // P
 UNITS = DIRECTIONS * H_BLOCKS
+SQUARE = 32
 
 FLOPS = 2 * ROWS * FEATURES * 3 * HIDDEN * DIRECTIONS
 BYTES = (
@@ -111,7 +112,7 @@ def tile_lstmnetwork_pa_e_kernel(tc, x, w_ih_words, w_ih_scales, b_ih, b_hh, out
         bias_cols = keep.tile([P, 32], F32)
         nc.vector.tensor_copy(out=bias_cols[:], in_=flipped_bias[:, 0:32])
 
-        out_blocks = out.rearrange("(r p) n -> p r n", p=P)
+        out_squares = out.rearrange("(b i) n -> i b n", i=SQUARE)
         sums = {}
         parts = {}
 
@@ -144,7 +145,7 @@ def tile_lstmnetwork_pa_e_kernel(tc, x, w_ih_words, w_ih_scales, b_ih, b_hh, out
             parts[unit, name] = result
 
         def product(unit, name, left, right):
-            result = work.tile([P, ROWS], F32, name=name, tag=name)
+            result = work.tile([P, ROWS], F32, name=name, tag=name, align_bytes=64)
             nc.vector.tensor_tensor(
                 out=result[:], in0=parts[unit, left][:], in1=parts[unit, right][:], op=ALU.mult
             )
@@ -161,22 +162,21 @@ def tile_lstmnetwork_pa_e_kernel(tc, x, w_ih_words, w_ih_scales, b_ih, b_hh, out
             parts[unit, "tanh_c"] = tanh_c
             product(unit, "hidden", "sig_o", "tanh_c")
 
-        def turn(unit):
-            flipped_h = flip_banks.tile([P, ROW_BLOCKS, P], F32, tag="flip")
-            for r in range(ROW_BLOCKS):
-                nc.tensor.transpose(
-                    flipped_h[:, r, :], parts[unit, "hidden"][:, P * r : P * (r + 1)], identity[:]
+        def turn_and_store(unit):
+            h_blocks = work.tile([P, ROWS], F32, align_bytes=64)
+            nc.vector.transpose(out=h_blocks[:], in_=parts[unit, "hidden"][:])
+            for a in range(P // SQUARE):
+                first_col = P * unit + SQUARE * a
+                nc.sync.dma_start(
+                    out=out_squares[:, :, first_col : first_col + SQUARE],
+                    in_=h_blocks[SQUARE * a : SQUARE * (a + 1), :].rearrange("i (b j) -> i b j", j=SQUARE),
                 )
-            parts[unit, "flipped_h"] = flipped_h
-
-        def store(unit):
-            h_rows = work.tile([P, ROW_BLOCKS, P], F32)
-            nc.vector.tensor_copy(out=h_rows[:], in_=parts[unit, "flipped_h"][:])
-            nc.sync.dma_start(out=out_blocks[:, :, P * unit : P * (unit + 1)], in_=h_rows[:])
 
         multiply(0)
         multiply(1)
         for step in range(UNITS + 2):
+            if step >= 2:
+                turn_and_store(step - 2)
             if step < UNITS:
                 cell_state(step)
             if 1 <= step <= UNITS:
@@ -185,7 +185,3 @@ def tile_lstmnetwork_pa_e_kernel(tc, x, w_ih_words, w_ih_scales, b_ih, b_hh, out
                 squash(step, GATE_O, ACT.Sigmoid, "sig_o")
             if step + 2 < UNITS:
                 multiply(step + 2)
-            if 1 <= step <= UNITS:
-                turn(step - 1)
-            if step >= 2:
-                store(step - 2)

@@ -25,7 +25,6 @@ GATE_COLS = 4 * HIDDEN
 GATE_I, GATE_G, GATE_O = 0, 2, 3
 H_BLOCKS = HIDDEN // P
 UNITS = DIRECTIONS * H_BLOCKS
-SQUARE = 32
 
 FLOPS = 2 * ROWS * FEATURES * 3 * HIDDEN * DIRECTIONS
 BYTES = (
@@ -67,11 +66,10 @@ def tile_lstmnetwork_pa_e_kernel(tc, x, w_ih_words, w_ih_scales, b_ih, b_hh, out
         w_words = keep.tile([P, DIRECTIONS * PASSES, 2 * GATE_COLS], U8, align_bytes=64)
         for d in range(DIRECTIONS):
             groups = slice(PASSES * d, PASSES * (d + 1))
-            for q in range(8):
-                first = 32 * (q // 4) + q % 4
+            for r in range(4):
                 nc.sync.dma_start(
-                    out=w_scales[first:P:64, groups, :].bitcast(I32),
-                    in_=w_ih_scales[groups, q:16:8, :].rearrange("g q n -> q g n").bitcast(I32),
+                    out=w_scales[r:P:32, groups, :].bitcast(I32),
+                    in_=w_ih_scales[groups, r:16:4, :].rearrange("g q n -> q g n").bitcast(I32),
                 )
             for first_gate, last_gate in ((GATE_I, GATE_I), (GATE_G, GATE_O)):
                 some_bytes = slice(2 * HIDDEN * first_gate, 2 * HIDDEN * (last_gate + 1))
@@ -112,7 +110,7 @@ def tile_lstmnetwork_pa_e_kernel(tc, x, w_ih_words, w_ih_scales, b_ih, b_hh, out
         bias_cols = keep.tile([P, 32], F32)
         nc.vector.tensor_copy(out=bias_cols[:], in_=flipped_bias[:, 0:32])
 
-        out_squares = out.rearrange("(b i) n -> i b n", i=SQUARE)
+        out_blocks = out.rearrange("(r p) n -> p r n", p=P)
         sums = {}
         parts = {}
 
@@ -145,7 +143,7 @@ def tile_lstmnetwork_pa_e_kernel(tc, x, w_ih_words, w_ih_scales, b_ih, b_hh, out
             parts[unit, name] = result
 
         def product(unit, name, left, right):
-            result = work.tile([P, ROWS], F32, name=name, tag=name, align_bytes=64)
+            result = work.tile([P, ROWS], F32, name=name, tag=name)
             nc.vector.tensor_tensor(
                 out=result[:], in0=parts[unit, left][:], in1=parts[unit, right][:], op=ALU.mult
             )
@@ -162,21 +160,22 @@ def tile_lstmnetwork_pa_e_kernel(tc, x, w_ih_words, w_ih_scales, b_ih, b_hh, out
             parts[unit, "tanh_c"] = tanh_c
             product(unit, "hidden", "sig_o", "tanh_c")
 
-        def turn_and_store(unit):
-            h_blocks = work.tile([P, ROWS], F32, align_bytes=64)
-            nc.vector.transpose(out=h_blocks[:], in_=parts[unit, "hidden"][:])
-            for a in range(P // SQUARE):
-                first_col = P * unit + SQUARE * a
-                nc.sync.dma_start(
-                    out=out_squares[:, :, first_col : first_col + SQUARE],
-                    in_=h_blocks[SQUARE * a : SQUARE * (a + 1), :].rearrange("i (b j) -> i b j", j=SQUARE),
+        def turn(unit):
+            flipped_h = flip_banks.tile([P, ROW_BLOCKS, P], F32, tag="flip")
+            for r in range(ROW_BLOCKS):
+                nc.tensor.transpose(
+                    flipped_h[:, r, :], parts[unit, "hidden"][:, P * r : P * (r + 1)], identity[:]
                 )
+            parts[unit, "flipped_h"] = flipped_h
+
+        def store(unit):
+            h_rows = work.tile([P, ROW_BLOCKS, P], F32)
+            nc.vector.tensor_copy(out=h_rows[:], in_=parts[unit, "flipped_h"][:])
+            nc.sync.dma_start(out=out_blocks[:, :, P * unit : P * (unit + 1)], in_=h_rows[:])
 
         multiply(0)
         multiply(1)
         for step in range(UNITS + 2):
-            if step >= 2:
-                turn_and_store(step - 2)
             if step < UNITS:
                 cell_state(step)
             if 1 <= step <= UNITS:
@@ -185,3 +184,7 @@ def tile_lstmnetwork_pa_e_kernel(tc, x, w_ih_words, w_ih_scales, b_ih, b_hh, out
                 squash(step, GATE_O, ACT.Sigmoid, "sig_o")
             if step + 2 < UNITS:
                 multiply(step + 2)
+            if 1 <= step <= UNITS:
+                turn(step - 1)
+            if step >= 2:
+                store(step - 2)

@@ -49,8 +49,11 @@ def tile_lstmnetwork_pa_e_kernel(tc, x, w_ih_words, w_ih_scales, b_ih, b_hh, out
         nc.vector.memset(bias_rows[:], 0.0)
         table_warmer = keep.tile([P, 1], F32)
         nc.vector.memset(table_warmer[:], 0.0)
-        w_scales = keep.tile([P, DIRECTIONS * PASSES, GATE_COLS], U8, align_bytes=64)
-        nc.vector.memset(w_scales[:].bitcast(I32), 0)
+        w_scales = []
+        for d in range(DIRECTIONS):
+            planes = keep.tile([P, PASSES, GATE_COLS], U8, name="w_scales%d" % d, align_bytes=64)
+            nc.vector.memset(planes[:].bitcast(I32), 0)
+            w_scales.append(planes)
 
         nc.scalar.dma_start(out=bias_rows[0:32, 0, :], in_=b_ih.rearrange("d (s p) -> (d s) p", p=P))
         nc.scalar.dma_start(out=bias_rows[0:32, 1, :], in_=b_hh.rearrange("d (s p) -> (d s) p", p=P))
@@ -59,24 +62,28 @@ def tile_lstmnetwork_pa_e_kernel(tc, x, w_ih_words, w_ih_scales, b_ih, b_hh, out
         identity = keep.tile([P, P], F32)
         make_identity(nc, identity[:])
 
-        x_rows = keep.tile([P, ROW_BLOCKS, FEATURES], BF16)
+        x_rows = []
         for r in range(ROW_BLOCKS):
-            nc.sync.dma_start(out=x_rows[:, r, :], in_=x[r])
+            block = keep.tile([P, FEATURES], BF16, name="x_rows%d" % r)
+            nc.sync.dma_start(out=block[:], in_=x[r])
+            x_rows.append(block)
 
-        w_words = keep.tile([P, DIRECTIONS * PASSES, 2 * GATE_COLS], U8, align_bytes=64)
+        w_words = {}
         for d in range(DIRECTIONS):
             groups = slice(PASSES * d, PASSES * (d + 1))
             for r in range(4):
                 nc.sync.dma_start(
-                    out=w_scales[r:P:32, groups, :].bitcast(I32),
+                    out=w_scales[d][r:P:32, :, :].bitcast(I32),
                     in_=w_ih_scales[groups, r:16:4, :].rearrange("g q n -> q g n").bitcast(I32),
                 )
-            for first_gate, last_gate in ((GATE_I, GATE_I), (GATE_G, GATE_O)):
-                some_bytes = slice(2 * HIDDEN * first_gate, 2 * HIDDEN * (last_gate + 1))
+            for gate in (GATE_I, GATE_G, GATE_O):
+                codes = keep.tile([P, PASSES, 2 * HIDDEN], U8, name="w_words%d_%d" % (d, gate), align_bytes=64)
+                some_bytes = slice(2 * HIDDEN * gate, 2 * HIDDEN * (gate + 1))
                 nc.sync.dma_start(
-                    out=w_words[:, groups, some_bytes].bitcast(I32),
+                    out=codes[:].bitcast(I32),
                     in_=w_ih_words[groups, :, some_bytes].rearrange("g p b -> p g b").bitcast(I32),
                 )
+                w_words[d, gate] = codes
 
         bias_sum_rows = keep.tile([P, P], F32)
         nc.vector.tensor_tensor(
@@ -86,19 +93,26 @@ def tile_lstmnetwork_pa_e_kernel(tc, x, w_ih_words, w_ih_scales, b_ih, b_hh, out
         x_grouped = keep.tile([P, PASSES, ROWS, 4], BF16, align_bytes=64)
         x_codes = keep.tile([P, PASSES, ROWS], U32, align_bytes=64)
         x_scales = keep.tile([P, PASSES, ROWS], U8, align_bytes=64)
+        head_banks = [(gate_banks, "gate%d" % g) for g in (GATE_I, GATE_G, GATE_O)] + [(flip_banks, "flip")]
         for r in range(ROW_BLOCKS):
             rows = slice(P * r, P * (r + 1))
-            word_cols = x_rows[:, r, :].bitcast(F32)
+            word_cols = x_rows[r][:].bitcast(F32)
+            flipped = []
             for c in range(PASSES):
-                flipped_x = flip_banks.tile([P, 2, P], F32, tag="flip")
+                pool, tag = head_banks[(PASSES * r + c) % len(head_banks)]
+                flipped_x = pool.tile([P, 2, P], F32, name="flipped_x", tag=tag)
                 for u in range(2):
                     nc.tensor.transpose(
                         flipped_x[:, u, :], word_cols[:, 256 * c + u : 256 * (c + 1) : 2], identity[:]
                     )
-                nc.scalar.copy(
-                    out=x_grouped[:, c, rows, :].bitcast(F32),
-                    in_=flipped_x[:].rearrange("p u r -> p r u"),
-                )
+                flipped.append(flipped_x)
+            nc.scalar.copy(
+                out=x_grouped[:, 0, rows, :].bitcast(F32), in_=flipped[0][:].rearrange("p u r -> p r u")
+            )
+            nc.vector.tensor_copy(
+                out=x_grouped[:, 1, rows, :].bitcast(F32), in_=flipped[1][:].rearrange("p u r -> p r u")
+            )
+            for c in range(PASSES):
                 nc.vector.quantize_mx(
                     out=x_codes[:, c, rows].bitcast(FP8X4),
                     scales=x_scales[:, c, rows],
@@ -125,11 +139,10 @@ def tile_lstmnetwork_pa_e_kernel(tc, x, w_ih_words, w_ih_scales, b_ih, b_hh, out
                 n0 = HIDDEN * gate + P * j
                 bank = gate_banks.tile([P, ROWS], F32, name="bank", tag="gate%d" % gate)
                 for c in range(PASSES):
-                    g = PASSES * d + c
                     nc.tensor.matmul_mx(
                         out=bank[:],
-                        lhsT=w_words[:, g, 2 * n0 : 2 * (n0 + P)].bitcast(FP4X4),
-                        lhsT_scale=w_scales[:, g, n0 : n0 + P],
+                        lhsT=w_words[d, gate][:, c, 2 * P * j : 2 * P * (j + 1)].bitcast(FP4X4),
+                        lhsT_scale=w_scales[d][:, c, n0 : n0 + P],
                         rhs=x_codes[:, c, :].bitcast(FP8X4),
                         rhs_scale=x_scales[:, c, :],
                         start=(c == 0),

@@ -24,6 +24,7 @@ HIDDEN = 512
 GATE_COLS = 4 * HIDDEN
 GATE_I, GATE_G, GATE_O = 0, 2, 3
 H_BLOCKS = HIDDEN // P
+WARM_UP = 6
 UNITS = DIRECTIONS * H_BLOCKS
 
 FLOPS = 2 * ROWS * FEATURES * 3 * HIDDEN * DIRECTIONS
@@ -44,6 +45,16 @@ def tile_lstmnetwork_pa_e_kernel(tc, x, w_ih_words, w_ih_scales, b_ih, b_hh, out
         work = stack.enter_context(tc.tile_pool(name="work", bufs=3))
         gate_banks = stack.enter_context(tc.psum_pool(name="gate_banks", bufs=2))
         flip_banks = stack.enter_context(tc.psum_pool(name="flip_banks", bufs=2))
+
+        zeros = keep.tile([P, ROWS], BF16)
+        nc.vector.memset(zeros[:], 0.0)
+        idle_bank = flip_banks.tile([P, ROWS], F32, tag="flip")
+
+        def keep_clock_up(times):
+            for i in range(times):
+                nc.tensor.matmul(idle_bank[:], lhsT=zeros[:, 0:P], rhs=zeros[:], start=True, stop=True)
+
+        keep_clock_up(WARM_UP)
 
         bias_rows = keep.tile([P, 2, P], BF16)
         nc.vector.memset(bias_rows[:], 0.0)
@@ -93,19 +104,21 @@ def tile_lstmnetwork_pa_e_kernel(tc, x, w_ih_words, w_ih_scales, b_ih, b_hh, out
         x_grouped = keep.tile([P, PASSES, ROWS, 4], BF16, align_bytes=64)
         x_codes = keep.tile([P, PASSES, ROWS], U32, align_bytes=64)
         x_scales = keep.tile([P, PASSES, ROWS], U8, align_bytes=64)
-        head_banks = [(gate_banks, "gate%d" % g) for g in (GATE_I, GATE_G, GATE_O)] + [(flip_banks, "flip")]
+        head_banks = 2 * [(gate_banks, "gate%d" % g) for g in (GATE_I, GATE_G, GATE_O)] + 2 * [(flip_banks, "flip")]
         for r in range(ROW_BLOCKS):
             rows = slice(P * r, P * (r + 1))
             word_cols = x_rows[r][:].bitcast(F32)
             flipped = []
             for c in range(PASSES):
-                pool, tag = head_banks[(PASSES * r + c) % len(head_banks)]
+                pool, tag = head_banks[PASSES * r + c]
                 flipped_x = pool.tile([P, 2, P], F32, name="flipped_x", tag=tag)
                 for u in range(2):
                     nc.tensor.transpose(
                         flipped_x[:, u, :], word_cols[:, 256 * c + u : 256 * (c + 1) : 2], identity[:]
                     )
                 flipped.append(flipped_x)
+            if r < ROW_BLOCKS - 1:
+                keep_clock_up(1)
             nc.scalar.copy(
                 out=x_grouped[:, 0, rows, :].bitcast(F32), in_=flipped[0][:].rearrange("p u r -> p r u")
             )

@@ -25,6 +25,7 @@ GATE_COLS = 4 * HIDDEN
 GATE_I, GATE_G, GATE_O = 0, 2, 3
 H_BLOCKS = HIDDEN // P
 WARM_UP = 6
+BRIDGE = 3
 UNITS = DIRECTIONS * H_BLOCKS
 
 FLOPS = 2 * ROWS * FEATURES * 3 * HIDDEN * DIRECTIONS
@@ -104,7 +105,8 @@ def tile_lstmnetwork_pa_e_kernel(tc, x, w_ih_words, w_ih_scales, b_ih, b_hh, out
         x_grouped = keep.tile([P, PASSES, ROWS, 4], BF16, align_bytes=64)
         x_codes = keep.tile([P, PASSES, ROWS], U32, align_bytes=64)
         x_scales = keep.tile([P, PASSES, ROWS], U8, align_bytes=64)
-        head_banks = 2 * [(gate_banks, "gate%d" % g) for g in (GATE_I, GATE_G, GATE_O)] + 2 * [(flip_banks, "flip")]
+        head_banks = 2 * [(gate_banks, "gate%d" % g) for g in (GATE_I, GATE_G, GATE_O)]
+        head_banks = head_banks + [(flip_banks, "flip"), (gate_banks, "gate%d" % GATE_I)]
         for r in range(ROW_BLOCKS):
             rows = slice(P * r, P * (r + 1))
             word_cols = x_rows[r][:].bitcast(F32)
@@ -117,8 +119,7 @@ def tile_lstmnetwork_pa_e_kernel(tc, x, w_ih_words, w_ih_scales, b_ih, b_hh, out
                         flipped_x[:, u, :], word_cols[:, 256 * c + u : 256 * (c + 1) : 2], identity[:]
                     )
                 flipped.append(flipped_x)
-            if r < ROW_BLOCKS - 1:
-                keep_clock_up(1)
+            keep_clock_up(1 if r < ROW_BLOCKS - 1 else BRIDGE)
             nc.scalar.copy(
                 out=x_grouped[:, 0, rows, :].bitcast(F32), in_=flipped[0][:].rearrange("p u r -> p r u")
             )

@@ -83,12 +83,19 @@ def tile_lstmnetwork_pa_e_kernel(tc, x, w_ih_words, w_ih_scales, b_ih, b_hh, out
         w_words = {}
         for d in range(DIRECTIONS):
             groups = slice(PASSES * d, PASSES * (d + 1))
-            for r in range(4):
-                nc.sync.dma_start(
-                    out=w_scales[d][r:P:32, :, :].bitcast(I32),
-                    in_=w_ih_scales[groups, r:16:4, :].rearrange("g q n -> q g n").bitcast(I32),
-                )
+            def load_scales(first_gate, last_gate):
+                cols = slice(HIDDEN * first_gate, HIDDEN * (last_gate + 1))
+                for r in range(4):
+                    nc.sync.dma_start(
+                        out=w_scales[d][r:P:32, :, cols].bitcast(I32),
+                        in_=w_ih_scales[groups, r:16:4, cols].rearrange("g q n -> q g n").bitcast(I32),
+                    )
+
             for gate in (GATE_I, GATE_G, GATE_O):
+                if gate == GATE_I:
+                    load_scales(GATE_I, GATE_I)
+                if gate == GATE_G:
+                    load_scales(GATE_G, GATE_O)
                 codes = keep.tile([P, PASSES, 2 * HIDDEN], U8, name="w_words%d_%d" % (d, gate), align_bytes=64)
                 some_bytes = slice(2 * HIDDEN * gate, 2 * HIDDEN * (gate + 1))
                 nc.sync.dma_start(
@@ -123,7 +130,8 @@ def tile_lstmnetwork_pa_e_kernel(tc, x, w_ih_words, w_ih_scales, b_ih, b_hh, out
             nc.scalar.copy(
                 out=x_grouped[:, 0, rows, :].bitcast(F32), in_=flipped[0][:].rearrange("p u r -> p r u")
             )
-            nc.vector.tensor_copy(
+            second_copy = nc.vector.tensor_copy if r < 2 else nc.scalar.copy
+            second_copy(
                 out=x_grouped[:, 1, rows, :].bitcast(F32), in_=flipped[1][:].rearrange("p u r -> p r u")
             )
             for c in range(PASSES):

@@ -24,8 +24,8 @@ HIDDEN = 512
 GATE_COLS = 4 * HIDDEN
 GATE_I, GATE_G, GATE_O = 0, 2, 3
 H_BLOCKS = HIDDEN // P
-WARM_UP = 6
-BRIDGE = 3
+WARM_UP = 5
+BRIDGE = 2
 UNITS = DIRECTIONS * H_BLOCKS
 
 FLOPS = 2 * ROWS * FEATURES * 3 * HIDDEN * DIRECTIONS
@@ -126,6 +126,9 @@ def tile_lstmnetwork_pa_e_kernel(tc, x, w_ih_words, w_ih_scales, b_ih, b_hh, out
                         flipped_x[:, u, :], word_cols[:, 256 * c + u : 256 * (c + 1) : 2], identity[:]
                     )
                 flipped.append(flipped_x)
+            if r == ROW_BLOCKS - 1:
+                flipped_bias = gate_banks.tile([P, P], F32, name="flipped_bias", tag="gate%d" % GATE_G)
+                nc.tensor.transpose(flipped_bias[:], bias_sum_rows[:], identity[:])
             keep_clock_up(1 if r < ROW_BLOCKS - 1 else BRIDGE)
             nc.scalar.copy(
                 out=x_grouped[:, 0, rows, :].bitcast(F32), in_=flipped[0][:].rearrange("p u r -> p r u")
@@ -141,8 +144,6 @@ def tile_lstmnetwork_pa_e_kernel(tc, x, w_ih_words, w_ih_scales, b_ih, b_hh, out
                     in_=x_grouped[:, c, rows, :].rearrange("p r t -> p (r t)"),
                 )
 
-        flipped_bias = flip_banks.tile([P, P], F32, tag="flip")
-        nc.tensor.transpose(flipped_bias[:], bias_sum_rows[:], identity[:])
         bias_cols = keep.tile([P, 32], F32)
         nc.vector.tensor_copy(out=bias_cols[:], in_=flipped_bias[:, 0:32])
 

@@ -156,9 +156,9 @@ def tile_lstmnetwork_pa_e_kernel(tc, x, w_ih_words, w_ih_scales, b_ih, b_hh, out
             col = 16 * d + 4 * gate + j
             return bias_cols[:, col : col + 1]
 
-        def multiply(unit):
+        def multiply(unit, gates=(GATE_I, GATE_G, GATE_O)):
             d, j = divmod(unit, H_BLOCKS)
-            for gate in (GATE_I, GATE_G, GATE_O):
+            for gate in gates:
                 n0 = HIDDEN * gate + P * j
                 bank = gate_banks.tile([P, ROWS], F32, name="bank", tag="gate%d" % gate)
                 for c in range(PASSES):
@@ -209,9 +209,21 @@ def tile_lstmnetwork_pa_e_kernel(tc, x, w_ih_words, w_ih_scales, b_ih, b_hh, out
             nc.vector.tensor_copy(out=h_rows[:], in_=parts[unit, "flipped_h"][:])
             nc.sync.dma_start(out=out_blocks[:, :, P * unit : P * (unit + 1)], in_=h_rows[:])
 
-        multiply(0)
-        multiply(1)
-        for step in range(UNITS + 2):
+        for gate in (GATE_I, GATE_G, GATE_O):
+            multiply(0, (gate,))
+            multiply(1, (gate,))
+        squash(0, GATE_I, ACT.Sigmoid, "sig_i")
+        squash(1, GATE_I, ACT.Sigmoid, "sig_i")
+        for unit in (0, 1):
+            squash(unit, GATE_G, ACT.Tanh, "tanh_g")
+            product(unit, "cell", "sig_i", "tanh_g")
+        squash(0, GATE_O, ACT.Sigmoid, "sig_o")
+        multiply(2)
+        hidden_state(0)
+        squash(1, GATE_O, ACT.Sigmoid, "sig_o")
+        multiply(3)
+        turn(0)
+        for step in range(2, UNITS + 2):
             if step < UNITS:
                 cell_state(step)
             if 1 <= step <= UNITS:

@@ -223,9 +223,16 @@ def tile_lstmnetwork_pa_e_kernel(tc, x, w_ih_words, w_ih_scales, b_ih, b_hh, out
         squash(1, GATE_O, ACT.Sigmoid, "sig_o")
         multiply(3)
         turn(0)
+        def idle_matmul(gate):
+            bank = gate_banks.tile([P, ROWS], F32, name="idle", tag="gate%d" % gate)
+            nc.tensor.matmul(bank[:], lhsT=zeros[:, 0:P], rhs=zeros[:], start=True, stop=True)
+
         for step in range(2, UNITS + 2):
             if step < UNITS:
                 cell_state(step)
+            if UNITS - 2 <= step < UNITS:
+                idle_matmul(GATE_I)
+                idle_matmul(GATE_G)
             if 1 <= step <= UNITS:
                 hidden_state(step - 1)
             if step < UNITS:
@@ -234,5 +241,10 @@ def tile_lstmnetwork_pa_e_kernel(tc, x, w_ih_words, w_ih_scales, b_ih, b_hh, out
                 multiply(step + 2)
             if 1 <= step <= UNITS:
                 turn(step - 1)
+            if UNITS - 2 <= step < UNITS:
+                idle_matmul(GATE_O)
+            if step == UNITS - 1:
+                idle_matmul(GATE_I)
+                idle_matmul(GATE_G)
             if step >= 2:
                 store(step - 2)

@@ -25,7 +25,6 @@ GATE_COLS = 4 * HIDDEN
 GATE_I, GATE_G, GATE_O = 0, 2, 3
 H_BLOCKS = HIDDEN // P
 WARM_UP = 5
-BRIDGE = 2
 UNITS = DIRECTIONS * H_BLOCKS
 
 FLOPS = 2 * ROWS * FEATURES * 3 * HIDDEN * DIRECTIONS
@@ -43,7 +42,7 @@ def tile_lstmnetwork_pa_e_kernel(tc, x, w_ih_words, w_ih_scales, b_ih, b_hh, out
     with ExitStack() as stack:
         stack.enter_context(tc.manual_schedule())
         keep = stack.enter_context(tc.tile_pool(name="keep", bufs=1))
-        work = stack.enter_context(tc.tile_pool(name="work", bufs=3))
+        work = stack.enter_context(tc.tile_pool(name="work", bufs=4))
         gate_banks = stack.enter_context(tc.psum_pool(name="gate_banks", bufs=2))
         flip_banks = stack.enter_context(tc.psum_pool(name="flip_banks", bufs=2))
 
@@ -61,11 +60,15 @@ def tile_lstmnetwork_pa_e_kernel(tc, x, w_ih_words, w_ih_scales, b_ih, b_hh, out
         nc.vector.memset(bias_rows[:], 0.0)
         table_warmer = keep.tile([P, 1], F32)
         nc.vector.memset(table_warmer[:], 0.0)
+        o_bias_rows = keep.tile([P, DIRECTIONS, HIDDEN], BF16)
+        nc.vector.memset(o_bias_rows[:].rearrange("p d n -> p (d n)").bitcast(I32), 0)
         w_scales = []
         for d in range(DIRECTIONS):
             planes = keep.tile([P, PASSES, GATE_COLS], U8, name="w_scales%d" % d, align_bytes=64)
             nc.vector.memset(planes[:].bitcast(I32), 0)
             w_scales.append(planes)
+        ones = keep.tile([P, P], BF16)
+        nc.vector.memset(ones[:], 1.0)
 
         nc.scalar.dma_start(out=bias_rows[0:32, 0, :], in_=b_ih.rearrange("d (s p) -> (d s) p", p=P))
         nc.scalar.dma_start(out=bias_rows[0:32, 1, :], in_=b_hh.rearrange("d (s p) -> (d s) p", p=P))
@@ -79,6 +82,9 @@ def tile_lstmnetwork_pa_e_kernel(tc, x, w_ih_words, w_ih_scales, b_ih, b_hh, out
             block = keep.tile([P, FEATURES], BF16, name="x_rows%d" % r)
             nc.sync.dma_start(out=block[:], in_=x[r])
             x_rows.append(block)
+        o_cols = slice(HIDDEN * GATE_O, HIDDEN * (GATE_O + 1))
+        nc.sync.dma_start(out=o_bias_rows[0:1, :, :], in_=b_ih[:, o_cols].rearrange("(o d) n -> o d n", o=1))
+        nc.sync.dma_start(out=o_bias_rows[1:2, :, :], in_=b_hh[:, o_cols].rearrange("(o d) n -> o d n", o=1))
 
         w_words = {}
         for d in range(DIRECTIONS):
@@ -129,7 +135,14 @@ def tile_lstmnetwork_pa_e_kernel(tc, x, w_ih_words, w_ih_scales, b_ih, b_hh, out
             if r == ROW_BLOCKS - 1:
                 flipped_bias = gate_banks.tile([P, P], F32, name="flipped_bias", tag="gate%d" % GATE_G)
                 nc.tensor.transpose(flipped_bias[:], bias_sum_rows[:], identity[:])
-            keep_clock_up(1 if r < ROW_BLOCKS - 1 else BRIDGE)
+            if r < ROW_BLOCKS - 1:
+                keep_clock_up(1)
+            else:
+                spread_banks = []
+                for d in range(DIRECTIONS):
+                    spread_bank = gate_banks.tile([P, HIDDEN], F32, name="spread_bank", tag="gate%d" % GATE_O)
+                    nc.tensor.matmul(spread_bank[:], lhsT=ones[:], rhs=o_bias_rows[:, d, :], start=True, stop=True)
+                    spread_banks.append(spread_bank)
             nc.scalar.copy(
                 out=x_grouped[:, 0, rows, :].bitcast(F32), in_=flipped[0][:].rearrange("p u r -> p r u")
             )
@@ -146,105 +159,171 @@ def tile_lstmnetwork_pa_e_kernel(tc, x, w_ih_words, w_ih_scales, b_ih, b_hh, out
 
         bias_cols = keep.tile([P, 32], F32)
         nc.vector.tensor_copy(out=bias_cols[:], in_=flipped_bias[:, 0:32])
+        bias_spread = keep.tile([P, DIRECTIONS, HIDDEN], F32)
+        for d in range(DIRECTIONS):
+            nc.vector.tensor_copy(out=bias_spread[:, d, :], in_=spread_banks[d][:])
 
         out_blocks = out.rearrange("(r p) n -> p r n", p=P)
         sums = {}
         parts = {}
+
+        def o_sums(unit):
+            d, j = divmod(unit, H_BLOCKS)
+            n0 = HIDDEN * GATE_O + P * j
+            bank = gate_banks.tile([P, ROW_BLOCKS, P], F32, name="o_bank", tag="gate%d" % GATE_O)
+            for r in range(ROW_BLOCKS):
+                rows = slice(P * r, P * (r + 1))
+                for c in range(PASSES):
+                    nc.tensor.matmul_mx(
+                        out=bank[:, r, :],
+                        lhsT=x_codes[:, c, rows].bitcast(FP8X4),
+                        lhsT_scale=x_scales[:, c, rows],
+                        rhs=w_words[d, GATE_O][:, c, 2 * P * j : 2 * P * (j + 1)].bitcast(FP4X4),
+                        rhs_scale=w_scales[d][:, c, n0 : n0 + P],
+                        start=(c == 0),
+                        stop=(c == PASSES - 1),
+                    )
+            sums[unit, GATE_O] = bank
+
+        def o_bias(unit):
+            d, j = divmod(unit, H_BLOCKS)
+            biased = work.tile([P, ROW_BLOCKS, P], F32, name="biased_o", tag="biased_o")
+            nc.vector.tensor_tensor(
+                out=biased[:],
+                in0=sums[unit, GATE_O][:],
+                in1=bias_spread[:, d : d + 1, P * j : P * (j + 1)].to_broadcast([P, ROW_BLOCKS, P]),
+                op=ALU.add,
+            )
+            parts[unit, "biased_o"] = biased
+
+        def o_gate(unit):
+            sig_o = work.tile([P, ROW_BLOCKS, P], F32, name="sig_o", tag="sig_o")
+            nc.scalar.activation(out=sig_o[:], in_=parts[unit, "biased_o"][:], func=ACT.Sigmoid)
+            parts[unit, "sig_o"] = sig_o
 
         def bias_of(unit, gate):
             d, j = divmod(unit, H_BLOCKS)
             col = 16 * d + 4 * gate + j
             return bias_cols[:, col : col + 1]
 
-        def multiply(unit, gates=(GATE_I, GATE_G, GATE_O)):
+        def multiply(unit, gate):
             d, j = divmod(unit, H_BLOCKS)
-            for gate in gates:
-                n0 = HIDDEN * gate + P * j
-                bank = gate_banks.tile([P, ROWS], F32, name="bank", tag="gate%d" % gate)
-                for c in range(PASSES):
-                    nc.tensor.matmul_mx(
-                        out=bank[:],
-                        lhsT=w_words[d, gate][:, c, 2 * P * j : 2 * P * (j + 1)].bitcast(FP4X4),
-                        lhsT_scale=w_scales[d][:, c, n0 : n0 + P],
-                        rhs=x_codes[:, c, :].bitcast(FP8X4),
-                        rhs_scale=x_scales[:, c, :],
-                        start=(c == 0),
-                        stop=(c == PASSES - 1),
-                    )
-                sums[unit, gate] = bank
+            n0 = HIDDEN * gate + P * j
+            bank = gate_banks.tile([P, ROWS], F32, name="bank", tag="gate%d" % gate)
+            for c in range(PASSES):
+                nc.tensor.matmul_mx(
+                    out=bank[:],
+                    lhsT=w_words[d, gate][:, c, 2 * P * j : 2 * P * (j + 1)].bitcast(FP4X4),
+                    lhsT_scale=w_scales[d][:, c, n0 : n0 + P],
+                    rhs=x_codes[:, c, :].bitcast(FP8X4),
+                    rhs_scale=x_scales[:, c, :],
+                    start=(c == 0),
+                    stop=(c == PASSES - 1),
+                )
+            sums[unit, gate] = bank
 
         def squash(unit, gate, func, name):
             result = work.tile([P, ROWS], F32, name=name, tag=name)
             nc.scalar.activation(out=result[:], in_=sums[unit, gate][:], func=func, bias=bias_of(unit, gate))
             parts[unit, name] = result
 
-        def product(unit, name, left, right):
-            result = work.tile([P, ROWS], F32, name=name, tag=name)
-            nc.vector.tensor_tensor(
-                out=result[:], in0=parts[unit, left][:], in1=parts[unit, right][:], op=ALU.mult
-            )
-            parts[unit, name] = result
+        def pieces_of(pieces):
+            return [slice(ROWS // pieces * n, ROWS // pieces * (n + 1)) for n in range(pieces)]
 
-        def cell_state(unit):
+        def cell(unit, pieces=1):
+            result = work.tile([P, ROWS], F32, name="cell", tag="cell")
+            for cols in pieces_of(pieces):
+                nc.vector.tensor_tensor(
+                    out=result[:, cols], in0=parts[unit, "sig_i"][:, cols], in1=parts[unit, "tanh_g"][:, cols], op=ALU.mult
+                )
+            parts[unit, "cell"] = result
+
+        def cell_state(unit, pieces=1):
             squash(unit, GATE_I, ACT.Sigmoid, "sig_i")
             squash(unit, GATE_G, ACT.Tanh, "tanh_g")
-            product(unit, "cell", "sig_i", "tanh_g")
+            cell(unit, pieces)
 
-        def hidden_state(unit):
-            tanh_c = work.tile([P, ROWS], F32)
-            nc.scalar.activation(out=tanh_c[:], in_=parts[unit, "cell"][:], func=ACT.Tanh)
-            parts[unit, "tanh_c"] = tanh_c
-            product(unit, "hidden", "sig_o", "tanh_c")
+        def halves(n):
+            if n is None:
+                return slice(0, ROWS), slice(0, ROW_BLOCKS)
+            return slice(ROWS // 2 * n, ROWS // 2 * (n + 1)), slice(ROW_BLOCKS // 2 * n, ROW_BLOCKS // 2 * (n + 1))
 
-        def turn(unit):
-            flipped_h = flip_banks.tile([P, ROW_BLOCKS, P], F32, tag="flip")
-            for r in range(ROW_BLOCKS):
-                nc.tensor.transpose(
-                    flipped_h[:, r, :], parts[unit, "hidden"][:, P * r : P * (r + 1)], identity[:]
-                )
-            parts[unit, "flipped_h"] = flipped_h
+        def squash_cell(unit, half=None):
+            cols, blocks = halves(half)
+            if (unit, "tanh_c") not in parts:
+                tanh_c = work.tile([P, ROWS], F32, name="tanh_c", tag="tanh_c")
+                parts[unit, "tanh_c"] = tanh_c
+            nc.scalar.activation(out=parts[unit, "tanh_c"][:, cols], in_=parts[unit, "cell"][:, cols], func=ACT.Tanh)
 
-        def store(unit):
-            h_rows = work.tile([P, ROW_BLOCKS, P], F32)
-            nc.vector.tensor_copy(out=h_rows[:], in_=parts[unit, "flipped_h"][:])
-            nc.sync.dma_start(out=out_blocks[:, :, P * unit : P * (unit + 1)], in_=h_rows[:])
+        def turn(unit, half=None, gate=None):
+            cols, blocks = halves(half)
+            count = blocks.stop - blocks.start
+            if gate is None:
+                flipped_c = flip_banks.tile([P, count, P], F32, name="flipped_c", tag="flip")
+            else:
+                flipped_c = gate_banks.tile([P, count, P], F32, name="flipped_c", tag="gate%d" % gate)
+            for r in range(count):
+                b = blocks.start + r
+                nc.tensor.transpose(flipped_c[:, r, :], parts[unit, "tanh_c"][:, P * b : P * (b + 1)], identity[:])
+            parts[unit, "flipped", half] = flipped_c
 
-        for gate in (GATE_I, GATE_G, GATE_O):
-            multiply(0, (gate,))
-            multiply(1, (gate,))
-        squash(0, GATE_I, ACT.Sigmoid, "sig_i")
-        squash(1, GATE_I, ACT.Sigmoid, "sig_i")
-        for unit in (0, 1):
-            squash(unit, GATE_G, ACT.Tanh, "tanh_g")
-            product(unit, "cell", "sig_i", "tanh_g")
-        squash(0, GATE_O, ACT.Sigmoid, "sig_o")
-        multiply(2)
-        hidden_state(0)
-        squash(1, GATE_O, ACT.Sigmoid, "sig_o")
-        multiply(3)
-        turn(0)
+        def hidden(unit, half=None):
+            d, j = divmod(unit, H_BLOCKS)
+            cols, blocks = halves(half)
+            h_rows = work.tile([P, blocks.stop - blocks.start, P], F32, name="h_rows", tag="h_rows")
+            nc.vector.tensor_tensor(
+                out=h_rows[:], in0=parts[unit, "flipped", half][:], in1=parts[unit, "sig_o"][:, blocks, :], op=ALU.mult
+            )
+            nc.sync.dma_start(out=out_blocks[:, blocks, P * unit : P * (unit + 1)], in_=h_rows[:])
+
         def idle_matmul(gate):
             bank = gate_banks.tile([P, ROWS], F32, name="idle", tag="gate%d" % gate)
             nc.tensor.matmul(bank[:], lhsT=zeros[:, 0:P], rhs=zeros[:], start=True, stop=True)
 
-        for step in range(2, UNITS + 2):
-            if step < UNITS:
-                cell_state(step)
-            if UNITS - 2 <= step < UNITS:
+        def multiply_all(unit):
+            multiply(unit, GATE_I)
+            multiply(unit, GATE_G)
+            o_sums(unit)
+
+        for gate in (GATE_I, GATE_G):
+            multiply(0, gate)
+            multiply(1, gate)
+        o_sums(0)
+        o_sums(1)
+        squash(0, GATE_I, ACT.Sigmoid, "sig_i")
+        squash(1, GATE_I, ACT.Sigmoid, "sig_i")
+        for unit in (0, 1):
+            squash(unit, GATE_G, ACT.Tanh, "tanh_g")
+            cell(unit)
+            o_bias(unit)
+        squash_cell(0)
+        o_gate(0)
+        multiply_all(2)
+        squash_cell(1)
+        o_gate(1)
+        multiply_all(3)
+        turn(0)
+        o_bias(2)
+        for step in range(2, UNITS):
+            cell_state(step)
+            if step >= UNITS - 2:
                 idle_matmul(GATE_I)
                 idle_matmul(GATE_G)
-            if 1 <= step <= UNITS:
-                hidden_state(step - 1)
-            if step < UNITS:
-                squash(step, GATE_O, ACT.Sigmoid, "sig_o")
+            if step > 2:
+                squash_cell(step - 1)
+            o_gate(step)
             if step + 2 < UNITS:
-                multiply(step + 2)
-            if 1 <= step <= UNITS:
-                turn(step - 1)
-            if UNITS - 2 <= step < UNITS:
+                multiply_all(step + 2)
+            turn(step - 1)
+            if step >= UNITS - 2:
                 idle_matmul(GATE_O)
-            if step == UNITS - 1:
-                idle_matmul(GATE_I)
-                idle_matmul(GATE_G)
-            if step >= 2:
-                store(step - 2)
+            if step + 1 < UNITS:
+                o_bias(step + 1)
+            hidden(step - 2)
+        squash_cell(7, 0)
+        squash_cell(7, 1)
+        turn(7, 0, GATE_I)
+        turn(7, 1, GATE_G)
+        hidden(6)
+        hidden(7, 0)
+        hidden(7, 1)

@@ -25,6 +25,8 @@ GATE_COLS = 4 * HIDDEN
 GATE_I, GATE_G, GATE_O = 0, 2, 3
 H_BLOCKS = HIDDEN // P
 WARM_UP = 5
+BRIDGE = 1
+ROW_FORM_FROM = 4
 UNITS = DIRECTIONS * H_BLOCKS
 
 FLOPS = 2 * ROWS * FEATURES * 3 * HIDDEN * DIRECTIONS
@@ -60,8 +62,8 @@ def tile_lstmnetwork_pa_e_kernel(tc, x, w_ih_words, w_ih_scales, b_ih, b_hh, out
         nc.vector.memset(bias_rows[:], 0.0)
         table_warmer = keep.tile([P, 1], F32)
         nc.vector.memset(table_warmer[:], 0.0)
-        o_bias_rows = keep.tile([P, DIRECTIONS, HIDDEN], BF16)
-        nc.vector.memset(o_bias_rows[:].rearrange("p d n -> p (d n)").bitcast(I32), 0)
+        o_bias_rows = keep.tile([P, HIDDEN], BF16)
+        nc.vector.memset(o_bias_rows[:].bitcast(I32), 0)
         w_scales = []
         for d in range(DIRECTIONS):
             planes = keep.tile([P, PASSES, GATE_COLS], U8, name="w_scales%d" % d, align_bytes=64)
@@ -83,8 +85,8 @@ def tile_lstmnetwork_pa_e_kernel(tc, x, w_ih_words, w_ih_scales, b_ih, b_hh, out
             nc.sync.dma_start(out=block[:], in_=x[r])
             x_rows.append(block)
         o_cols = slice(HIDDEN * GATE_O, HIDDEN * (GATE_O + 1))
-        nc.sync.dma_start(out=o_bias_rows[0:1, :, :], in_=b_ih[:, o_cols].rearrange("(o d) n -> o d n", o=1))
-        nc.sync.dma_start(out=o_bias_rows[1:2, :, :], in_=b_hh[:, o_cols].rearrange("(o d) n -> o d n", o=1))
+        nc.sync.dma_start(out=o_bias_rows[0:1, :], in_=b_ih[1:2, o_cols])
+        nc.sync.dma_start(out=o_bias_rows[1:2, :], in_=b_hh[1:2, o_cols])
 
         w_words = {}
         for d in range(DIRECTIONS):
@@ -135,14 +137,10 @@ def tile_lstmnetwork_pa_e_kernel(tc, x, w_ih_words, w_ih_scales, b_ih, b_hh, out
             if r == ROW_BLOCKS - 1:
                 flipped_bias = gate_banks.tile([P, P], F32, name="flipped_bias", tag="gate%d" % GATE_G)
                 nc.tensor.transpose(flipped_bias[:], bias_sum_rows[:], identity[:])
-            if r < ROW_BLOCKS - 1:
-                keep_clock_up(1)
-            else:
-                spread_banks = []
-                for d in range(DIRECTIONS):
-                    spread_bank = gate_banks.tile([P, HIDDEN], F32, name="spread_bank", tag="gate%d" % GATE_O)
-                    nc.tensor.matmul(spread_bank[:], lhsT=ones[:], rhs=o_bias_rows[:, d, :], start=True, stop=True)
-                    spread_banks.append(spread_bank)
+            keep_clock_up(1 if r < ROW_BLOCKS - 1 else BRIDGE)
+            if r == ROW_BLOCKS - 1:
+                spread_bank = gate_banks.tile([P, HIDDEN], F32, name="spread_bank", tag="gate%d" % GATE_O)
+                nc.tensor.matmul(spread_bank[:], lhsT=ones[:], rhs=o_bias_rows[:], start=True, stop=True)
             nc.scalar.copy(
                 out=x_grouped[:, 0, rows, :].bitcast(F32), in_=flipped[0][:].rearrange("p u r -> p r u")
             )
@@ -159,171 +157,170 @@ def tile_lstmnetwork_pa_e_kernel(tc, x, w_ih_words, w_ih_scales, b_ih, b_hh, out
 
         bias_cols = keep.tile([P, 32], F32)
         nc.vector.tensor_copy(out=bias_cols[:], in_=flipped_bias[:, 0:32])
-        bias_spread = keep.tile([P, DIRECTIONS, HIDDEN], F32)
-        for d in range(DIRECTIONS):
-            nc.vector.tensor_copy(out=bias_spread[:, d, :], in_=spread_banks[d][:])
+        bias_spread = keep.tile([P, 1, HIDDEN], F32)
+        nc.vector.tensor_copy(out=bias_spread[:, 0, :], in_=spread_bank[:])
 
         out_blocks = out.rearrange("(r p) n -> p r n", p=P)
         sums = {}
         parts = {}
 
-        def o_sums(unit):
-            d, j = divmod(unit, H_BLOCKS)
-            n0 = HIDDEN * GATE_O + P * j
-            bank = gate_banks.tile([P, ROW_BLOCKS, P], F32, name="o_bank", tag="gate%d" % GATE_O)
-            for r in range(ROW_BLOCKS):
-                rows = slice(P * r, P * (r + 1))
-                for c in range(PASSES):
-                    nc.tensor.matmul_mx(
-                        out=bank[:, r, :],
-                        lhsT=x_codes[:, c, rows].bitcast(FP8X4),
-                        lhsT_scale=x_scales[:, c, rows],
-                        rhs=w_words[d, GATE_O][:, c, 2 * P * j : 2 * P * (j + 1)].bitcast(FP4X4),
-                        rhs_scale=w_scales[d][:, c, n0 : n0 + P],
-                        start=(c == 0),
-                        stop=(c == PASSES - 1),
-                    )
-            sums[unit, GATE_O] = bank
-
-        def o_bias(unit):
-            d, j = divmod(unit, H_BLOCKS)
-            biased = work.tile([P, ROW_BLOCKS, P], F32, name="biased_o", tag="biased_o")
-            nc.vector.tensor_tensor(
-                out=biased[:],
-                in0=sums[unit, GATE_O][:],
-                in1=bias_spread[:, d : d + 1, P * j : P * (j + 1)].to_broadcast([P, ROW_BLOCKS, P]),
-                op=ALU.add,
-            )
-            parts[unit, "biased_o"] = biased
-
-        def o_gate(unit):
-            sig_o = work.tile([P, ROW_BLOCKS, P], F32, name="sig_o", tag="sig_o")
-            nc.scalar.activation(out=sig_o[:], in_=parts[unit, "biased_o"][:], func=ACT.Sigmoid)
-            parts[unit, "sig_o"] = sig_o
+        def row_form(unit):
+            return unit >= ROW_FORM_FROM
 
         def bias_of(unit, gate):
             d, j = divmod(unit, H_BLOCKS)
             col = 16 * d + 4 * gate + j
             return bias_cols[:, col : col + 1]
 
-        def multiply(unit, gate):
+        def multiply(unit, gates=(GATE_I, GATE_G, GATE_O)):
             d, j = divmod(unit, H_BLOCKS)
-            n0 = HIDDEN * gate + P * j
-            bank = gate_banks.tile([P, ROWS], F32, name="bank", tag="gate%d" % gate)
-            for c in range(PASSES):
-                nc.tensor.matmul_mx(
-                    out=bank[:],
-                    lhsT=w_words[d, gate][:, c, 2 * P * j : 2 * P * (j + 1)].bitcast(FP4X4),
-                    lhsT_scale=w_scales[d][:, c, n0 : n0 + P],
-                    rhs=x_codes[:, c, :].bitcast(FP8X4),
-                    rhs_scale=x_scales[:, c, :],
-                    start=(c == 0),
-                    stop=(c == PASSES - 1),
-                )
-            sums[unit, gate] = bank
+            for gate in gates:
+                n0 = HIDDEN * gate + P * j
+                w_codes = w_words[d, gate][:, :, 2 * P * j : 2 * P * (j + 1)]
+                w_planes = w_scales[d][:, :, n0 : n0 + P]
+                bank = gate_banks.tile([P, ROWS], F32, name="bank", tag="gate%d" % gate)
+                if gate == GATE_O and row_form(unit):
+                    for r in range(ROW_BLOCKS):
+                        rows = slice(P * r, P * (r + 1))
+                        for c in range(PASSES):
+                            nc.tensor.matmul_mx(
+                                out=bank[:, rows],
+                                lhsT=x_codes[:, c, rows].bitcast(FP8X4),
+                                lhsT_scale=x_scales[:, c, rows],
+                                rhs=w_codes[:, c, :].bitcast(FP4X4),
+                                rhs_scale=w_planes[:, c, :],
+                                start=(c == 0),
+                                stop=(c == PASSES - 1),
+                            )
+                else:
+                    for c in range(PASSES):
+                        nc.tensor.matmul_mx(
+                            out=bank[:],
+                            lhsT=w_codes[:, c, :].bitcast(FP4X4),
+                            lhsT_scale=w_planes[:, c, :],
+                            rhs=x_codes[:, c, :].bitcast(FP8X4),
+                            rhs_scale=x_scales[:, c, :],
+                            start=(c == 0),
+                            stop=(c == PASSES - 1),
+                        )
+                sums[unit, gate] = bank
 
         def squash(unit, gate, func, name):
             result = work.tile([P, ROWS], F32, name=name, tag=name)
             nc.scalar.activation(out=result[:], in_=sums[unit, gate][:], func=func, bias=bias_of(unit, gate))
             parts[unit, name] = result
 
-        def pieces_of(pieces):
-            return [slice(ROWS // pieces * n, ROWS // pieces * (n + 1)) for n in range(pieces)]
+        def product(unit, name, left, right):
+            result = work.tile([P, ROWS], F32, name=name, tag=name)
+            nc.vector.tensor_tensor(
+                out=result[:], in0=parts[unit, left][:], in1=parts[unit, right][:], op=ALU.mult
+            )
+            parts[unit, name] = result
 
-        def cell(unit, pieces=1):
-            result = work.tile([P, ROWS], F32, name="cell", tag="cell")
-            for cols in pieces_of(pieces):
-                nc.vector.tensor_tensor(
-                    out=result[:, cols], in0=parts[unit, "sig_i"][:, cols], in1=parts[unit, "tanh_g"][:, cols], op=ALU.mult
-                )
-            parts[unit, "cell"] = result
-
-        def cell_state(unit, pieces=1):
+        def cell_state(unit):
             squash(unit, GATE_I, ACT.Sigmoid, "sig_i")
             squash(unit, GATE_G, ACT.Tanh, "tanh_g")
-            cell(unit, pieces)
+            product(unit, "cell", "sig_i", "tanh_g")
 
-        def halves(n):
-            if n is None:
-                return slice(0, ROWS), slice(0, ROW_BLOCKS)
-            return slice(ROWS // 2 * n, ROWS // 2 * (n + 1)), slice(ROW_BLOCKS // 2 * n, ROW_BLOCKS // 2 * (n + 1))
+        def add_o_bias(unit):
+            j = unit % H_BLOCKS
+            biased = work.tile([P, ROW_BLOCKS, P], F32, name="biased_o", tag="biased_o")
+            nc.vector.tensor_tensor(
+                out=biased[:],
+                in0=sums[unit, GATE_O][:].rearrange("p (r n) -> p r n", n=P),
+                in1=bias_spread[:, :, P * j : P * (j + 1)].to_broadcast([P, ROW_BLOCKS, P]),
+                op=ALU.add,
+            )
+            parts[unit, "biased_o"] = biased
 
-        def squash_cell(unit, half=None):
-            cols, blocks = halves(half)
+        def o_gate(unit):
+            if row_form(unit):
+                sig_o = work.tile([P, ROWS], F32, name="sig_o", tag="sig_o")
+                nc.scalar.activation(
+                    out=sig_o[:], in_=parts[unit, "biased_o"][:].rearrange("p r n -> p (r n)"), func=ACT.Sigmoid
+                )
+                parts[unit, "sig_o"] = sig_o
+            else:
+                squash(unit, GATE_O, ACT.Sigmoid, "sig_o")
+
+        def some_rows(half):
+            if half is None:
+                return slice(0, ROWS)
+            return slice(ROWS // 2 * half, ROWS // 2 * (half + 1))
+
+        def hidden_state(unit, half=None):
+            cols = some_rows(half)
             if (unit, "tanh_c") not in parts:
                 tanh_c = work.tile([P, ROWS], F32, name="tanh_c", tag="tanh_c")
                 parts[unit, "tanh_c"] = tanh_c
             nc.scalar.activation(out=parts[unit, "tanh_c"][:, cols], in_=parts[unit, "cell"][:, cols], func=ACT.Tanh)
+            if not row_form(unit):
+                product(unit, "hidden", "sig_o", "tanh_c")
 
         def turn(unit, half=None, gate=None):
-            cols, blocks = halves(half)
-            count = blocks.stop - blocks.start
+            cols = some_rows(half)
             if gate is None:
-                flipped_c = flip_banks.tile([P, count, P], F32, name="flipped_c", tag="flip")
+                flipped = flip_banks.tile([P, ROWS], F32, name="flipped", tag="flip")
             else:
-                flipped_c = gate_banks.tile([P, count, P], F32, name="flipped_c", tag="gate%d" % gate)
-            for r in range(count):
-                b = blocks.start + r
-                nc.tensor.transpose(flipped_c[:, r, :], parts[unit, "tanh_c"][:, P * b : P * (b + 1)], identity[:])
-            parts[unit, "flipped", half] = flipped_c
+                flipped = gate_banks.tile([P, ROWS], F32, name="flipped", tag="gate%d" % gate)
+            source = parts[unit, "tanh_c" if row_form(unit) else "hidden"]
+            for first in range(cols.start, cols.stop, P):
+                nc.tensor.transpose(flipped[:, first : first + P], source[:, first : first + P], identity[:])
+            parts[unit, "flipped", half] = flipped
 
-        def hidden(unit, half=None):
-            d, j = divmod(unit, H_BLOCKS)
-            cols, blocks = halves(half)
-            h_rows = work.tile([P, blocks.stop - blocks.start, P], F32, name="h_rows", tag="h_rows")
-            nc.vector.tensor_tensor(
-                out=h_rows[:], in0=parts[unit, "flipped", half][:], in1=parts[unit, "sig_o"][:, blocks, :], op=ALU.mult
+        def store(unit, half=None):
+            cols = some_rows(half)
+            h_rows = work.tile([P, ROWS], F32, name="h_rows", tag="h_rows")
+            if row_form(unit):
+                nc.vector.tensor_tensor(
+                    out=h_rows[:, cols], in0=parts[unit, "flipped", half][:, cols], in1=parts[unit, "sig_o"][:, cols], op=ALU.mult
+                )
+            else:
+                nc.vector.tensor_copy(out=h_rows[:, cols], in_=parts[unit, "flipped", half][:, cols])
+            nc.sync.dma_start(
+                out=out_blocks[:, cols.start // P : cols.stop // P, P * unit : P * (unit + 1)],
+                in_=h_rows[:, cols].rearrange("p (r n) -> p r n", n=P),
             )
-            nc.sync.dma_start(out=out_blocks[:, blocks, P * unit : P * (unit + 1)], in_=h_rows[:])
+
+        for gate in (GATE_I, GATE_G, GATE_O):
+            multiply(0, (gate,))
+            multiply(1, (gate,))
+        squash(0, GATE_I, ACT.Sigmoid, "sig_i")
+        squash(1, GATE_I, ACT.Sigmoid, "sig_i")
+        for unit in (0, 1):
+            squash(unit, GATE_G, ACT.Tanh, "tanh_g")
+            product(unit, "cell", "sig_i", "tanh_g")
+        o_gate(0)
+        multiply(2)
+        hidden_state(0)
+        o_gate(1)
+        multiply(3)
+        turn(0)
 
         def idle_matmul(gate):
             bank = gate_banks.tile([P, ROWS], F32, name="idle", tag="gate%d" % gate)
             nc.tensor.matmul(bank[:], lhsT=zeros[:, 0:P], rhs=zeros[:], start=True, stop=True)
 
-        def multiply_all(unit):
-            multiply(unit, GATE_I)
-            multiply(unit, GATE_G)
-            o_sums(unit)
-
-        for gate in (GATE_I, GATE_G):
-            multiply(0, gate)
-            multiply(1, gate)
-        o_sums(0)
-        o_sums(1)
-        squash(0, GATE_I, ACT.Sigmoid, "sig_i")
-        squash(1, GATE_I, ACT.Sigmoid, "sig_i")
-        for unit in (0, 1):
-            squash(unit, GATE_G, ACT.Tanh, "tanh_g")
-            cell(unit)
-            o_bias(unit)
-        squash_cell(0)
-        o_gate(0)
-        multiply_all(2)
-        squash_cell(1)
-        o_gate(1)
-        multiply_all(3)
-        turn(0)
-        o_bias(2)
         for step in range(2, UNITS):
             cell_state(step)
             if step >= UNITS - 2:
                 idle_matmul(GATE_I)
                 idle_matmul(GATE_G)
-            if step > 2:
-                squash_cell(step - 1)
+            hidden_state(step - 1)
             o_gate(step)
             if step + 2 < UNITS:
-                multiply_all(step + 2)
+                multiply(step + 2)
             turn(step - 1)
             if step >= UNITS - 2:
                 idle_matmul(GATE_O)
-            if step + 1 < UNITS:
-                o_bias(step + 1)
-            hidden(step - 2)
-        squash_cell(7, 0)
-        squash_cell(7, 1)
-        turn(7, 0, GATE_I)
-        turn(7, 1, GATE_G)
-        hidden(6)
-        hidden(7, 0)
-        hidden(7, 1)
+            if step + 1 < UNITS and row_form(step + 1):
+                add_o_bias(step + 1)
+            store(step - 2)
+        last = UNITS - 1
+        hidden_state(last, 0)
+        hidden_state(last, 1)
+        turn(last, 0, GATE_I)
+        turn(last, 1, GATE_G)
+        store(last - 1)
+        store(last, 0)
+        store(last, 1)

from contextlib import ExitStack

import concourse.mybir as mybir
from concourse.masks import make_identity

F32 = mybir.dt.float32
BF16 = mybir.dt.bfloat16
I32 = mybir.dt.int32
U32 = mybir.dt.uint32
U8 = mybir.dt.uint8
FP8X4 = mybir.dt.float8_e4m3fn_x4
FP4X4 = mybir.dt.float4_e2m1fn_x4
ACT = mybir.ActivationFunctionType
ALU = mybir.AluOpType

P = 128
ROW_BLOCKS = 4
ROWS = ROW_BLOCKS * P
FEATURES = 1024
K_PASS = 4 * P
PASSES = FEATURES // K_PASS
DIRECTIONS = 2
HIDDEN = 512
GATE_COLS = 4 * HIDDEN
GATE_I, GATE_G, GATE_O = 0, 2, 3
H_BLOCKS = HIDDEN // P
WARM_UP = 5
BRIDGE = 1
ROW_FORM_FROM = 4
UNITS = DIRECTIONS * H_BLOCKS

FLOPS = 2 * ROWS * FEATURES * 3 * HIDDEN * DIRECTIONS
BYTES = (
    ROWS * FEATURES * 2
    + DIRECTIONS * FEATURES * 3 * HIDDEN // 2
    + DIRECTIONS * FEATURES * 3 * HIDDEN // 32
    + 2 * DIRECTIONS * 3 * HIDDEN * 2
    + ROWS * DIRECTIONS * HIDDEN * 4
)


def tile_lstmnetwork_pa_e_kernel(tc, x, w_ih_words, w_ih_scales, b_ih, b_hh, out):
    nc = tc.nc
    with ExitStack() as stack:
        stack.enter_context(tc.manual_schedule())
        keep = stack.enter_context(tc.tile_pool(name="keep", bufs=1))
        work = stack.enter_context(tc.tile_pool(name="work", bufs=4))
        gate_banks = stack.enter_context(tc.psum_pool(name="gate_banks", bufs=2))
        flip_banks = stack.enter_context(tc.psum_pool(name="flip_banks", bufs=2))

        zeros = keep.tile([P, ROWS], BF16)
        nc.vector.memset(zeros[:], 0.0)
        idle_bank = flip_banks.tile([P, ROWS], F32, tag="flip")

        def keep_clock_up(times):
            for i in range(times):
                nc.tensor.matmul(idle_bank[:], lhsT=zeros[:, 0:P], rhs=zeros[:], start=True, stop=True)

        keep_clock_up(WARM_UP)

        bias_rows = keep.tile([P, 2, P], BF16)
        nc.vector.memset(bias_rows[:], 0.0)
        table_warmer = keep.tile([P, 1], F32)
        nc.vector.memset(table_warmer[:], 0.0)
        o_bias_rows = keep.tile([P, HIDDEN], BF16)
        nc.vector.memset(o_bias_rows[:].bitcast(I32), 0)
        w_scales = []
        for d in range(DIRECTIONS):
            planes = keep.tile([P, PASSES, GATE_COLS], U8, name="w_scales%d" % d, align_bytes=64)
            nc.vector.memset(planes[:].bitcast(I32), 0)
            w_scales.append(planes)
        ones = keep.tile([P, P], BF16)
        nc.vector.memset(ones[:], 1.0)

        nc.scalar.dma_start(out=bias_rows[0:32, 0, :], in_=b_ih.rearrange("d (s p) -> (d s) p", p=P))
        nc.scalar.dma_start(out=bias_rows[0:32, 1, :], in_=b_hh.rearrange("d (s p) -> (d s) p", p=P))
        nc.scalar.activation(out=table_warmer[:], in_=table_warmer[:], func=ACT.Sigmoid)

        identity = keep.tile([P, P], F32)
        make_identity(nc, identity[:])

        x_rows = []
        for r in range(ROW_BLOCKS):
            block = keep.tile([P, FEATURES], BF16, name="x_rows%d" % r)
            nc.sync.dma_start(out=block[:], in_=x[r])
            x_rows.append(block)
        o_cols = slice(HIDDEN * GATE_O, HIDDEN * (GATE_O + 1))
        nc.sync.dma_start(out=o_bias_rows[0:1, :], in_=b_ih[1:2, o_cols])
        nc.sync.dma_start(out=o_bias_rows[1:2, :], in_=b_hh[1:2, o_cols])

        w_words = {}
        for d in range(DIRECTIONS):
            groups = slice(PASSES * d, PASSES * (d + 1))
            def load_scales(first_gate, last_gate):
                cols = slice(HIDDEN * first_gate, HIDDEN * (last_gate + 1))
                for r in range(4):
                    nc.sync.dma_start(
                        out=w_scales[d][r:P:32, :, cols].bitcast(I32),
                        in_=w_ih_scales[groups, r:16:4, cols].rearrange("g q n -> q g n").bitcast(I32),
                    )

            for gate in (GATE_I, GATE_G, GATE_O):
                if gate == GATE_I:
                    load_scales(GATE_I, GATE_I)
                if gate == GATE_G:
                    load_scales(GATE_G, GATE_O)
                codes = keep.tile([P, PASSES, 2 * HIDDEN], U8, name="w_words%d_%d" % (d, gate), align_bytes=64)
                some_bytes = slice(2 * HIDDEN * gate, 2 * HIDDEN * (gate + 1))
                nc.sync.dma_start(
                    out=codes[:].bitcast(I32),
                    in_=w_ih_words[groups, :, some_bytes].rearrange("g p b -> p g b").bitcast(I32),
                )
                w_words[d, gate] = codes

        bias_sum_rows = keep.tile([P, P], F32)
        nc.vector.tensor_tensor(
            out=bias_sum_rows[:], in0=bias_rows[:, 0, :], in1=bias_rows[:, 1, :], op=ALU.add
        )

        x_grouped = keep.tile([P, PASSES, ROWS, 4], BF16, align_bytes=64)
        x_codes = keep.tile([P, PASSES, ROWS], U32, align_bytes=64)
        x_scales = keep.tile([P, PASSES, ROWS], U8, align_bytes=64)
        head_banks = 2 * [(gate_banks, "gate%d" % g) for g in (GATE_I, GATE_G, GATE_O)]
        head_banks = head_banks + [(flip_banks, "flip"), (gate_banks, "gate%d" % GATE_I)]
        for r in range(ROW_BLOCKS):
            rows = slice(P * r, P * (r + 1))
            word_cols = x_rows[r][:].bitcast(F32)
            flipped = []
            for c in range(PASSES):
                pool, tag = head_banks[PASSES * r + c]
                flipped_x = pool.tile([P, 2, P], F32, name="flipped_x", tag=tag)
                for u in range(2):
                    nc.tensor.transpose(
                        flipped_x[:, u, :], word_cols[:, 256 * c + u : 256 * (c + 1) : 2], identity[:]
                    )
                flipped.append(flipped_x)
            if r == ROW_BLOCKS - 1:
                flipped_bias = gate_banks.tile([P, P], F32, name="flipped_bias", tag="gate%d" % GATE_G)
                nc.tensor.transpose(flipped_bias[:], bias_sum_rows[:], identity[:])
            keep_clock_up(1 if r < ROW_BLOCKS - 1 else BRIDGE)
            if r == ROW_BLOCKS - 1:
                spread_bank = gate_banks.tile([P, HIDDEN], F32, name="spread_bank", tag="gate%d" % GATE_O)
                nc.tensor.matmul(spread_bank[:], lhsT=ones[:], rhs=o_bias_rows[:], start=True, stop=True)
            nc.scalar.copy(
                out=x_grouped[:, 0, rows, :].bitcast(F32), in_=flipped[0][:].rearrange("p u r -> p r u")
            )
            second_copy = nc.vector.tensor_copy if r < 2 else nc.scalar.copy
            second_copy(
                out=x_grouped[:, 1, rows, :].bitcast(F32), in_=flipped[1][:].rearrange("p u r -> p r u")
            )
            for c in range(PASSES):
                nc.vector.quantize_mx(
                    out=x_codes[:, c, rows].bitcast(FP8X4),
                    scales=x_scales[:, c, rows],
                    in_=x_grouped[:, c, rows, :].rearrange("p r t -> p (r t)"),
                )

        bias_cols = keep.tile([P, 32], F32)
        nc.vector.tensor_copy(out=bias_cols[:], in_=flipped_bias[:, 0:32])
        bias_spread = keep.tile([P, 1, HIDDEN], F32)
        nc.vector.tensor_copy(out=bias_spread[:, 0, :], in_=spread_bank[:])

        out_blocks = out.rearrange("(r p) n -> p r n", p=P)
        sums = {}
        parts = {}

        def row_form(unit):
            return unit >= ROW_FORM_FROM

        def bias_of(unit, gate):
            d, j = divmod(unit, H_BLOCKS)
            col = 16 * d + 4 * gate + j
            return bias_cols[:, col : col + 1]

        def multiply(unit, gates=(GATE_I, GATE_G, GATE_O)):
            d, j = divmod(unit, H_BLOCKS)
            for gate in gates:
                n0 = HIDDEN * gate + P * j
                w_codes = w_words[d, gate][:, :, 2 * P * j : 2 * P * (j + 1)]
                w_planes = w_scales[d][:, :, n0 : n0 + P]
                bank = gate_banks.tile([P, ROWS], F32, name="bank", tag="gate%d" % gate)
                if gate == GATE_O and row_form(unit):
                    for r in range(ROW_BLOCKS):
                        rows = slice(P * r, P * (r + 1))
                        for c in range(PASSES):
                            nc.tensor.matmul_mx(
                                out=bank[:, rows],
                                lhsT=x_codes[:, c, rows].bitcast(FP8X4),
                                lhsT_scale=x_scales[:, c, rows],
                                rhs=w_codes[:, c, :].bitcast(FP4X4),
                                rhs_scale=w_planes[:, c, :],
                                start=(c == 0),
                                stop=(c == PASSES - 1),
                            )
                else:
                    for c in range(PASSES):
                        nc.tensor.matmul_mx(
                            out=bank[:],
                            lhsT=w_codes[:, c, :].bitcast(FP4X4),
                            lhsT_scale=w_planes[:, c, :],
                            rhs=x_codes[:, c, :].bitcast(FP8X4),
                            rhs_scale=x_scales[:, c, :],
                            start=(c == 0),
                            stop=(c == PASSES - 1),
                        )
                sums[unit, gate] = bank

        def squash(unit, gate, func, name):
            result = work.tile([P, ROWS], F32, name=name, tag=name)
            nc.scalar.activation(out=result[:], in_=sums[unit, gate][:], func=func, bias=bias_of(unit, gate))
            parts[unit, name] = result

        def product(unit, name, left, right):
            result = work.tile([P, ROWS], F32, name=name, tag=name)
            nc.vector.tensor_tensor(
                out=result[:], in0=parts[unit, left][:], in1=parts[unit, right][:], op=ALU.mult
            )
            parts[unit, name] = result

        def cell_state(unit):
            squash(unit, GATE_I, ACT.Sigmoid, "sig_i")
            squash(unit, GATE_G, ACT.Tanh, "tanh_g")
            product(unit, "cell", "sig_i", "tanh_g")

        def add_o_bias(unit):
            j = unit % H_BLOCKS
            biased = work.tile([P, ROW_BLOCKS, P], F32, name="biased_o", tag="biased_o")
            nc.vector.tensor_tensor(
                out=biased[:],
                in0=sums[unit, GATE_O][:].rearrange("p (r n) -> p r n", n=P),
                in1=bias_spread[:, :, P * j : P * (j + 1)].to_broadcast([P, ROW_BLOCKS, P]),
                op=ALU.add,
            )
            parts[unit, "biased_o"] = biased

        def o_gate(unit):
            if row_form(unit):
                sig_o = work.tile([P, ROWS], F32, name="sig_o", tag="sig_o")
                nc.scalar.activation(
                    out=sig_o[:], in_=parts[unit, "biased_o"][:].rearrange("p r n -> p (r n)"), func=ACT.Sigmoid
                )
                parts[unit, "sig_o"] = sig_o
            else:
                squash(unit, GATE_O, ACT.Sigmoid, "sig_o")

        def some_rows(half):
            if half is None:
                return slice(0, ROWS)
            return slice(ROWS // 2 * half, ROWS // 2 * (half + 1))

        def hidden_state(unit, half=None):
            cols = some_rows(half)
            if (unit, "tanh_c") not in parts:
                tanh_c = work.tile([P, ROWS], F32, name="tanh_c", tag="tanh_c")
                parts[unit, "tanh_c"] = tanh_c
            nc.scalar.activation(out=parts[unit, "tanh_c"][:, cols], in_=parts[unit, "cell"][:, cols], func=ACT.Tanh)
            if not row_form(unit):
                product(unit, "hidden", "sig_o", "tanh_c")

        def turn(unit, half=None, gate=None):
            cols = some_rows(half)
            if gate is None:
                flipped = flip_banks.tile([P, ROWS], F32, name="flipped", tag="flip")
            else:
                flipped = gate_banks.tile([P, ROWS], F32, name="flipped", tag="gate%d" % gate)
            source = parts[unit, "tanh_c" if row_form(unit) else "hidden"]
            for first in range(cols.start, cols.stop, P):
                nc.tensor.transpose(flipped[:, first : first + P], source[:, first : first + P], identity[:])
            parts[unit, "flipped", half] = flipped

        def store(unit, half=None):
            cols = some_rows(half)
            h_rows = work.tile([P, ROWS], F32, name="h_rows", tag="h_rows")
            if row_form(unit):
                nc.vector.tensor_tensor(
                    out=h_rows[:, cols], in0=parts[unit, "flipped", half][:, cols], in1=parts[unit, "sig_o"][:, cols], op=ALU.mult
                )
            else:
                nc.vector.tensor_copy(out=h_rows[:, cols], in_=parts[unit, "flipped", half][:, cols])
            nc.sync.dma_start(
                out=out_blocks[:, cols.start // P : cols.stop // P, P * unit : P * (unit + 1)],
                in_=h_rows[:, cols].rearrange("p (r n) -> p r n", n=P),
            )

        for gate in (GATE_I, GATE_G, GATE_O):
            multiply(0, (gate,))
            multiply(1, (gate,))
        squash(0, GATE_I, ACT.Sigmoid, "sig_i")
        squash(1, GATE_I, ACT.Sigmoid, "sig_i")
        for unit in (0, 1):
            squash(unit, GATE_G, ACT.Tanh, "tanh_g")
            product(unit, "cell", "sig_i", "tanh_g")
        o_gate(0)
        multiply(2)
        hidden_state(0)
        o_gate(1)
        multiply(3)
        turn(0)

        def idle_matmul(gate):
            bank = gate_banks.tile([P, ROWS], F32, name="idle", tag="gate%d" % gate)
            nc.tensor.matmul(bank[:], lhsT=zeros[:, 0:P], rhs=zeros[:], start=True, stop=True)

        for step in range(2, UNITS):
            cell_state(step)
            if step >= UNITS - 2:
                idle_matmul(GATE_I)
                idle_matmul(GATE_G)
            hidden_state(step - 1)
            o_gate(step)
            if step + 2 < UNITS:
                multiply(step + 2)
            turn(step - 1)
            if step >= UNITS - 2:
                idle_matmul(GATE_O)
            if step + 1 < UNITS and row_form(step + 1):
                add_o_bias(step + 1)
            store(step - 2)
        last = UNITS - 1
        hidden_state(last, 0)
        hidden_state(last, 1)
        turn(last, 0, GATE_I)
        turn(last, 1, GATE_G)
        store(last - 1)
        store(last, 0)
        store(last, 1)
